import numpy as np
import ml_dtypes

BF16 = ml_dtypes.bfloat16


def bf(x):
    return np.asarray(x, np.float32).astype(BF16)


def f32(x):
    return np.asarray(x, np.float32)


def f64(x):
    return np.asarray(x).astype(np.float64)


def striped(idx):
    return np.tile(idx.reshape(-1, 16).T, (8, 1))


C, S, N = 256, 4096, 2048
EPS = 1e-5
STD = 0.02


def setup_inputs():
    return {"table": f32(STD * np.random.standard_normal((C, S))), "offs": striped(np.random.permutation(np.tile(np.arange(S), 2))[:N])}


def reference(table, offs):
    idx = offs[:16].T.reshape(-1)
    x = f64(table)[:, idx]
    m = x.mean(axis=0, keepdims=True)
    d = x - m
    v = (d * d).mean(axis=0, keepdims=True)
    return d / np.sqrt(v + EPS)

@@ -1,0 +1,87 @@
+import concourse.mybir as mybir
+
+F32 = mybir.dt.float32
+BF16 = mybir.dt.bfloat16
+U16 = mybir.dt.uint16
+ACT = mybir.ActivationFunctionType
+ALU = mybir.AluOpType
+
+P = 128
+CHANNELS = 256
+BLOCKS = CHANNELS // P
+WORDS = 4096
+TOKENS = 2048
+PIECE = 512
+PIECES = TOKENS // PIECE
+EPS = 1e-5
+
+
+def tile_recurrentbdh_kernel(tc, table, offs, out):
+    nc = tc.nc
+    with (
+        tc.tile_pool(name="held", bufs=1) as held,
+        tc.tile_pool(name="work", bufs=PIECES) as work,
+        tc.psum_pool(name="psum", bufs=2) as psum,
+    ):
+        offsets = held.tile([P, TOKENS // 16], U16, name="offsets")
+        nc.sync.dma_start(offsets[:], offs)
+
+        windows = [held.tile([P, WORDS], F32, name=f"window{b}") for b in range(BLOCKS)]
+        half = WORDS // 2
+        for b in range(BLOCKS):
+            rows = table[b * P : (b + 1) * P, :]
+            nc.sync.dma_start(windows[b][:, :half], rows[:, :half])
+            nc.scalar.dma_start(windows[b][:, half:], rows[:, half:])
+
+        averager = held.tile([P, P], BF16, name="averager")
+        nc.vector.memset(averager[:], 1.0 / CHANNELS)
+        eps = held.tile([P, 1], F32, name="eps")
+        nc.vector.memset(eps[:], EPS)
+
+        warm = held.tile([P, 1], F32, name="warm")
+        nc.scalar.activation(warm[:], eps[:], ACT.Abs_reciprocal_sqrt)
+
+        def look_up(b, piece):
+            picked = work.tile([P, PIECE], F32, name=f"picked{b}")
+            columns = offsets[:, piece * (PIECE // 16) : (piece + 1) * (PIECE // 16)]
+            nc.scalar.activation(picked[:], windows[b][:].indirect(columns), ACT.Copy)
+            rounded = work.tile([P, PIECE], BF16, name=f"rounded{b}")
+            nc.vector.tensor_copy(rounded[:], picked[:])
+            return picked, rounded
+
+        first = [look_up(0, piece) for piece in range(PIECES)]
+
+        for piece in range(PIECES):
+            looked_up = [first[piece], look_up(1, piece)]
+
+            mean = psum.tile([P, PIECE], F32, name="mean")
+            for b in range(BLOCKS):
+                nc.tensor.matmul(
+                    mean[:], averager[:], looked_up[b][1][:], start=(b == 0), stop=(b == BLOCKS - 1)
+                )
+
+            centred = []
+            squares = []
+            for b in range(BLOCKS):
+                diff = work.tile([P, PIECE], F32, name=f"diff{b}")
+                nc.vector.tensor_tensor(diff[:], looked_up[b][0][:], mean[:], ALU.subtract)
+                square = work.tile([P, PIECE], BF16, name=f"square{b}")
+                nc.vector.tensor_tensor(square[:], diff[:], diff[:], ALU.mult)
+                centred.append(diff)
+                squares.append(square)
+
+            variance = psum.tile([P, PIECE], F32, name="variance")
+            for b in range(BLOCKS):
+                nc.tensor.matmul(
+                    variance[:], averager[:], squares[b][:], start=(b == 0), stop=(b == BLOCKS - 1)
+                )
+
+            rstd = work.tile([P, PIECE], F32, name="rstd")
+            nc.scalar.activation(rstd[:], variance[:], ACT.Abs_reciprocal_sqrt, bias=eps[:])
+
+            for b in range(BLOCKS):
+                normed = work.tile([P, PIECE], F32, name=f"normed{b}")
+                nc.vector.tensor_tensor(normed[:], centred[b][:], rstd[:], ALU.mult)
+                nc.sync.dma_start(
+                    out[b * P : (b + 1) * P, piece * PIECE : (piece + 1) * PIECE], normed[:]
+                )

@@ -21,7 +21,7 @@ def tile_recurrentbdh_kernel(tc, table, offs, out):
     with (
         tc.tile_pool(name="held", bufs=1) as held,
         tc.tile_pool(name="work", bufs=PIECES) as work,
-        tc.psum_pool(name="psum", bufs=2) as psum,
+        tc.psum_pool(name="psum", bufs=PIECES) as psum,
     ):
         offsets = held.tile([P, TOKENS // 16], U16, name="offsets")
         nc.sync.dma_start(offsets[:], offs)
@@ -66,7 +66,7 @@ def tile_recurrentbdh_kernel(tc, table, offs, out):
                 diff = work.tile([P, PIECE], F32, name=f"diff{b}")
                 nc.vector.tensor_tensor(diff[:], looked_up[b][0][:], mean[:], ALU.subtract)
                 square = work.tile([P, PIECE], BF16, name=f"square{b}")
-                nc.vector.tensor_tensor(square[:], diff[:], diff[:], ALU.mult)
+                nc.scalar.activation(square[:], diff[:], ACT.Square)
                 centred.append(diff)
                 squares.append(square)
 

@@ -33,55 +33,62 @@ def tile_recurrentbdh_kernel(tc, table, offs, out):
             nc.sync.dma_start(windows[b][:, :half], rows[:, :half])
             nc.scalar.dma_start(windows[b][:, half:], rows[:, half:])
 
-        averager = held.tile([P, P], BF16, name="averager")
+        averager = held.tile([P, P], F32, name="averager")
         nc.vector.memset(averager[:], 1.0 / CHANNELS)
+        averager_bf16 = held.tile([P, P], BF16, name="averager_bf16")
+        nc.vector.memset(averager_bf16[:], 1.0 / CHANNELS)
         eps = held.tile([P, 1], F32, name="eps")
         nc.vector.memset(eps[:], EPS)
 
         warm = held.tile([P, 1], F32, name="warm")
         nc.scalar.activation(warm[:], eps[:], ACT.Abs_reciprocal_sqrt)
 
+        picked = [[None] * PIECES for b in range(BLOCKS)]
+        mean = [None] * PIECES
+        diff = [[None] * PIECES for b in range(BLOCKS)]
+        variance = [None] * PIECES
+
         def look_up(b, piece):
-            picked = work.tile([P, PIECE], F32, name=f"picked{b}")
+            picked[b][piece] = work.tile([P, PIECE], F32, name=f"picked{b}")
             columns = offsets[:, piece * (PIECE // 16) : (piece + 1) * (PIECE // 16)]
-            nc.scalar.activation(picked[:], windows[b][:].indirect(columns), ACT.Copy)
-            rounded = work.tile([P, PIECE], BF16, name=f"rounded{b}")
-            nc.vector.tensor_copy(rounded[:], picked[:])
-            return picked, rounded
+            nc.scalar.activation(picked[b][piece][:], windows[b][:].indirect(columns), ACT.Copy)
+            if b == 0:
+                mean[piece] = psum.tile([P, PIECE], F32, name="mean")
+            nc.tensor.matmul(
+                mean[piece][:], averager[:], picked[b][piece][:], start=(b == 0), stop=(b == BLOCKS - 1)
+            )
 
-        first = [look_up(0, piece) for piece in range(PIECES)]
-
-        for piece in range(PIECES):
-            looked_up = [first[piece], look_up(1, piece)]
-
-            mean = psum.tile([P, PIECE], F32, name="mean")
+        def centre(piece):
             for b in range(BLOCKS):
-                nc.tensor.matmul(
-                    mean[:], averager[:], looked_up[b][1][:], start=(b == 0), stop=(b == BLOCKS - 1)
-                )
+                diff[b][piece] = work.tile([P, PIECE], F32, name=f"diff{b}")
+                nc.vector.tensor_tensor(diff[b][piece][:], picked[b][piece][:], mean[piece][:], ALU.subtract)
 
-            centred = []
-            squares = []
+        def spread(piece):
+            variance[piece] = psum.tile([P, PIECE], F32, name="variance")
             for b in range(BLOCKS):
-                diff = work.tile([P, PIECE], F32, name=f"diff{b}")
-                nc.vector.tensor_tensor(diff[:], looked_up[b][0][:], mean[:], ALU.subtract)
                 square = work.tile([P, PIECE], BF16, name=f"square{b}")
-                nc.scalar.activation(square[:], diff[:], ACT.Square)
-                centred.append(diff)
-                squares.append(square)
-
-            variance = psum.tile([P, PIECE], F32, name="variance")
-            for b in range(BLOCKS):
+                nc.scalar.activation(square[:], diff[b][piece][:], ACT.Square)
                 nc.tensor.matmul(
-                    variance[:], averager[:], squares[b][:], start=(b == 0), stop=(b == BLOCKS - 1)
+                    variance[piece][:], averager_bf16[:], square[:], start=(b == 0), stop=(b == BLOCKS - 1)
                 )
 
+        def normalise(piece):
             rstd = work.tile([P, PIECE], F32, name="rstd")
-            nc.scalar.activation(rstd[:], variance[:], ACT.Abs_reciprocal_sqrt, bias=eps[:])
-
+            nc.scalar.activation(rstd[:], variance[piece][:], ACT.Abs_reciprocal_sqrt, bias=eps[:])
             for b in range(BLOCKS):
                 normed = work.tile([P, PIECE], F32, name=f"normed{b}")
-                nc.vector.tensor_tensor(normed[:], centred[b][:], rstd[:], ALU.mult)
+                nc.vector.tensor_tensor(normed[:], diff[b][piece][:], rstd[:], ALU.mult)
                 nc.sync.dma_start(
                     out[b * P : (b + 1) * P, piece * PIECE : (piece + 1) * PIECE], normed[:]
                 )
+
+        for piece in range(PIECES):
+            look_up(0, piece)
+        for piece in range(PIECES):
+            look_up(1, piece)
+            centre(piece)
+        spread(0)
+        for piece in range(1, PIECES):
+            spread(piece)
+            normalise(piece - 1)
+        normalise(PIECES - 1)

@@ -11,8 +11,10 @@ CHANNELS = 256
 BLOCKS = CHANNELS // P
 WORDS = 4096
 TOKENS = 2048
-PIECE = 512
-PIECES = TOKENS // PIECE
+WIDTHS = (256, 512, 512, 512, 256)
+STARTS = tuple(sum(WIDTHS[:piece]) for piece in range(len(WIDTHS)))
+PIECES = len(WIDTHS)
+VARIANCE_BANKS = 8 - PIECES
 EPS = 1e-5
 
 
@@ -21,7 +23,8 @@ def tile_recurrentbdh_kernel(tc, table, offs, out):
     with (
         tc.tile_pool(name="held", bufs=1) as held,
         tc.tile_pool(name="work", bufs=PIECES) as work,
-        tc.psum_pool(name="psum", bufs=PIECES) as psum,
+        tc.psum_pool(name="psum_mean", bufs=PIECES) as psum_mean,
+        tc.psum_pool(name="psum_variance", bufs=VARIANCE_BANKS) as psum_variance,
     ):
         offsets = held.tile([P, TOKENS // 16], U16, name="offsets")
         nc.sync.dma_start(offsets[:], offs)
@@ -49,38 +52,41 @@ def tile_recurrentbdh_kernel(tc, table, offs, out):
         variance = [None] * PIECES
 
         def look_up(b, piece):
-            picked[b][piece] = work.tile([P, PIECE], F32, name=f"picked{b}")
-            columns = offsets[:, piece * (PIECE // 16) : (piece + 1) * (PIECE // 16)]
+            start, width = STARTS[piece], WIDTHS[piece]
+            picked[b][piece] = work.tile([P, width], F32, name=f"picked{b}")
+            columns = offsets[:, start // 16 : (start + width) // 16]
             nc.scalar.activation(picked[b][piece][:], windows[b][:].indirect(columns), ACT.Copy)
             if b == 0:
-                mean[piece] = psum.tile([P, PIECE], F32, name="mean")
+                mean[piece] = psum_mean.tile([P, width], F32, name="mean")
             nc.tensor.matmul(
                 mean[piece][:], averager[:], picked[b][piece][:], start=(b == 0), stop=(b == BLOCKS - 1)
             )
 
         def centre(piece):
             for b in range(BLOCKS):
-                diff[b][piece] = work.tile([P, PIECE], F32, name=f"diff{b}")
+                diff[b][piece] = work.tile([P, WIDTHS[piece]], F32, name=f"diff{b}")
                 nc.vector.tensor_tensor(diff[b][piece][:], picked[b][piece][:], mean[piece][:], ALU.subtract)
 
         def spread(piece):
-            variance[piece] = psum.tile([P, PIECE], F32, name="variance")
+            variance[piece] = psum_variance.tile([P, WIDTHS[piece]], F32, name="variance")
             for b in range(BLOCKS):
-                square = work.tile([P, PIECE], BF16, name=f"square{b}")
-                nc.scalar.activation(square[:], diff[b][piece][:], ACT.Square)
+                square = work.tile([P, WIDTHS[piece]], BF16, name=f"square{b}")
+                if piece == 0:
+                    nc.vector.tensor_tensor(square[:], diff[b][piece][:], diff[b][piece][:], ALU.mult)
+                else:
+                    nc.scalar.activation(square[:], diff[b][piece][:], ACT.Square)
                 nc.tensor.matmul(
                     variance[piece][:], averager_bf16[:], square[:], start=(b == 0), stop=(b == BLOCKS - 1)
                 )
 
         def normalise(piece):
-            rstd = work.tile([P, PIECE], F32, name="rstd")
+            start, width = STARTS[piece], WIDTHS[piece]
+            rstd = work.tile([P, width], F32, name="rstd")
             nc.scalar.activation(rstd[:], variance[piece][:], ACT.Abs_reciprocal_sqrt, bias=eps[:])
             for b in range(BLOCKS):
-                normed = work.tile([P, PIECE], F32, name=f"normed{b}")
+                normed = work.tile([P, width], F32, name=f"normed{b}")
                 nc.vector.tensor_tensor(normed[:], diff[b][piece][:], rstd[:], ALU.mult)
-                nc.sync.dma_start(
-                    out[b * P : (b + 1) * P, piece * PIECE : (piece + 1) * PIECE], normed[:]
-                )
+                nc.sync.dma_start(out[b * P : (b + 1) * P, start : start + width], normed[:])
 
         for piece in range(PIECES):
             look_up(0, piece)

@@ -73,6 +73,8 @@ def tile_recurrentbdh_kernel(tc, table, offs, out):
                 square = work.tile([P, WIDTHS[piece]], BF16, name=f"square{b}")
                 if piece == 0:
                     nc.vector.tensor_tensor(square[:], diff[b][piece][:], diff[b][piece][:], ALU.mult)
+                elif piece == 1 and b == 1:
+                    nc.gpsimd.tensor_tensor(square[:], diff[b][piece][:], diff[b][piece][:], ALU.mult)
                 else:
                     nc.scalar.activation(square[:], diff[b][piece][:], ACT.Square)
                 nc.tensor.matmul(

@@ -11,7 +11,7 @@ CHANNELS = 256
 BLOCKS = CHANNELS // P
 WORDS = 4096
 TOKENS = 2048
-WIDTHS = (256, 512, 512, 512, 256)
+WIDTHS = (256, 384, 384, 384, 384, 256)
 STARTS = tuple(sum(WIDTHS[:piece]) for piece in range(len(WIDTHS)))
 PIECES = len(WIDTHS)
 VARIANCE_BANKS = 8 - PIECES
@@ -58,9 +58,17 @@ def tile_recurrentbdh_kernel(tc, table, offs, out):
             nc.scalar.activation(picked[b][piece][:], windows[b][:].indirect(columns), ACT.Copy)
             if b == 0:
                 mean[piece] = psum_mean.tile([P, width], F32, name="mean")
-            nc.tensor.matmul(
-                mean[piece][:], averager[:], picked[b][piece][:], start=(b == 0), stop=(b == BLOCKS - 1)
-            )
+            if b == 0 and piece >= PIECES - 2:
+                rounded = work.tile([P, width], BF16, name="rounded")
+                nc.vector.tensor_copy(rounded[:], picked[0][piece][:])
+                remainder = work.tile([P, width], BF16, name="remainder")
+                nc.vector.tensor_tensor(remainder[:], picked[0][piece][:], rounded[:], ALU.subtract)
+                nc.tensor.matmul(mean[piece][:], averager_bf16[:], rounded[:], start=True, stop=False)
+                nc.tensor.matmul(mean[piece][:], averager_bf16[:], remainder[:], start=False, stop=False)
+            else:
+                nc.tensor.matmul(
+                    mean[piece][:], averager[:], picked[b][piece][:], start=(b == 0), stop=(b == BLOCKS - 1)
+                )
 
         def centre(piece):
             for b in range(BLOCKS):
@@ -71,9 +79,7 @@ def tile_recurrentbdh_kernel(tc, table, offs, out):
             variance[piece] = psum_variance.tile([P, WIDTHS[piece]], F32, name="variance")
             for b in range(BLOCKS):
                 square = work.tile([P, WIDTHS[piece]], BF16, name=f"square{b}")
-                if piece == 0:
-                    nc.vector.tensor_tensor(square[:], diff[b][piece][:], diff[b][piece][:], ALU.mult)
-                elif piece == 1 and b == 1:
+                if piece == 0 or (piece in (1, 2) and b == 1):
                     nc.gpsimd.tensor_tensor(square[:], diff[b][piece][:], diff[b][piece][:], ALU.mult)
                 else:
                     nc.scalar.activation(square[:], diff[b][piece][:], ACT.Square)

@@ -11,7 +11,7 @@ CHANNELS = 256
 BLOCKS = CHANNELS // P
 WORDS = 4096
 TOKENS = 2048
-WIDTHS = (256, 384, 384, 384, 384, 256)
+WIDTHS = (256, 512, 512, 512, 256)
 STARTS = tuple(sum(WIDTHS[:piece]) for piece in range(len(WIDTHS)))
 PIECES = len(WIDTHS)
 VARIANCE_BANKS = 8 - PIECES
@@ -56,19 +56,22 @@ def tile_recurrentbdh_kernel(tc, table, offs, out):
             picked[b][piece] = work.tile([P, width], F32, name=f"picked{b}")
             columns = offsets[:, start // 16 : (start + width) // 16]
             nc.scalar.activation(picked[b][piece][:], windows[b][:].indirect(columns), ACT.Copy)
-            if b == 0:
-                mean[piece] = psum_mean.tile([P, width], F32, name="mean")
-            if b == 0 and piece >= PIECES - 2:
+
+        def open_mean(piece):
+            width = WIDTHS[piece]
+            mean[piece] = psum_mean.tile([P, width], F32, name="mean")
+            if piece < PIECES - 2:
+                nc.tensor.matmul(mean[piece][:], averager[:], picked[0][piece][:], start=True, stop=False)
+            else:
                 rounded = work.tile([P, width], BF16, name="rounded")
                 nc.vector.tensor_copy(rounded[:], picked[0][piece][:])
                 remainder = work.tile([P, width], BF16, name="remainder")
                 nc.vector.tensor_tensor(remainder[:], picked[0][piece][:], rounded[:], ALU.subtract)
                 nc.tensor.matmul(mean[piece][:], averager_bf16[:], rounded[:], start=True, stop=False)
                 nc.tensor.matmul(mean[piece][:], averager_bf16[:], remainder[:], start=False, stop=False)
-            else:
-                nc.tensor.matmul(
-                    mean[piece][:], averager[:], picked[b][piece][:], start=(b == 0), stop=(b == BLOCKS - 1)
-                )
+
+        def close_mean(piece):
+            nc.tensor.matmul(mean[piece][:], averager[:], picked[1][piece][:], start=False, stop=True)
 
         def centre(piece):
             for b in range(BLOCKS):
@@ -79,7 +82,7 @@ def tile_recurrentbdh_kernel(tc, table, offs, out):
             variance[piece] = psum_variance.tile([P, WIDTHS[piece]], F32, name="variance")
             for b in range(BLOCKS):
                 square = work.tile([P, WIDTHS[piece]], BF16, name=f"square{b}")
-                if piece == 0 or (piece in (1, 2) and b == 1):
+                if piece == 0 or (piece == 1 and b == 1):
                     nc.gpsimd.tensor_tensor(square[:], diff[b][piece][:], diff[b][piece][:], ALU.mult)
                 else:
                     nc.scalar.activation(square[:], diff[b][piece][:], ACT.Square)
@@ -96,10 +99,16 @@ def tile_recurrentbdh_kernel(tc, table, offs, out):
                 nc.vector.tensor_tensor(normed[:], diff[b][piece][:], rstd[:], ALU.mult)
                 nc.sync.dma_start(out[b * P : (b + 1) * P, start : start + width], normed[:])
 
+        last = PIECES - 1
         for piece in range(PIECES):
             look_up(0, piece)
+            if piece < last:
+                open_mean(piece)
         for piece in range(PIECES):
             look_up(1, piece)
+            close_mean(piece)
+            if piece == 0:
+                open_mean(last)
             centre(piece)
         spread(0)
         for piece in range(1, PIECES):

@@ -82,7 +82,9 @@ def tile_recurrentbdh_kernel(tc, table, offs, out):
             variance[piece] = psum_variance.tile([P, WIDTHS[piece]], F32, name="variance")
             for b in range(BLOCKS):
                 square = work.tile([P, WIDTHS[piece]], BF16, name=f"square{b}")
-                if piece == 0 or (piece == 1 and b == 1):
+                if piece == 0:
+                    nc.vector.tensor_tensor(square[:], diff[b][piece][:], diff[b][piece][:], ALU.mult)
+                elif piece == 1 and b == 1:
                     nc.gpsimd.tensor_tensor(square[:], diff[b][piece][:], diff[b][piece][:], ALU.mult)
                 else:
                     nc.scalar.activation(square[:], diff[b][piece][:], ACT.Square)

@@ -30,11 +30,8 @@ def tile_recurrentbdh_kernel(tc, table, offs, out):
         nc.sync.dma_start(offsets[:], offs)
 
         windows = [held.tile([P, WORDS], F32, name=f"window{b}") for b in range(BLOCKS)]
-        half = WORDS // 2
         for b in range(BLOCKS):
-            rows = table[b * P : (b + 1) * P, :]
-            nc.sync.dma_start(windows[b][:, :half], rows[:, :half])
-            nc.scalar.dma_start(windows[b][:, half:], rows[:, half:])
+            nc.sync.dma_start(windows[b][:], table[b * P : (b + 1) * P, :])
 
         averager = held.tile([P, P], F32, name="averager")
         nc.vector.memset(averager[:], 1.0 / CHANNELS)

import concourse.mybir as mybir

F32 = mybir.dt.float32
BF16 = mybir.dt.bfloat16
U16 = mybir.dt.uint16
ACT = mybir.ActivationFunctionType
ALU = mybir.AluOpType

P = 128
CHANNELS = 256
BLOCKS = CHANNELS // P
WORDS = 4096
TOKENS = 2048
WIDTHS = (256, 512, 512, 512, 256)
STARTS = tuple(sum(WIDTHS[:piece]) for piece in range(len(WIDTHS)))
PIECES = len(WIDTHS)
VARIANCE_BANKS = 8 - PIECES
EPS = 1e-5


def tile_recurrentbdh_kernel(tc, table, offs, out):
    nc = tc.nc
    with (
        tc.tile_pool(name="held", bufs=1) as held,
        tc.tile_pool(name="work", bufs=PIECES) as work,
        tc.psum_pool(name="psum_mean", bufs=PIECES) as psum_mean,
        tc.psum_pool(name="psum_variance", bufs=VARIANCE_BANKS) as psum_variance,
    ):
        offsets = held.tile([P, TOKENS // 16], U16, name="offsets")
        nc.sync.dma_start(offsets[:], offs)

        windows = [held.tile([P, WORDS], F32, name=f"window{b}") for b in range(BLOCKS)]
        for b in range(BLOCKS):
            nc.sync.dma_start(windows[b][:], table[b * P : (b + 1) * P, :])

        averager = held.tile([P, P], F32, name="averager")
        nc.vector.memset(averager[:], 1.0 / CHANNELS)
        averager_bf16 = held.tile([P, P], BF16, name="averager_bf16")
        nc.vector.memset(averager_bf16[:], 1.0 / CHANNELS)
        eps = held.tile([P, 1], F32, name="eps")
        nc.vector.memset(eps[:], EPS)

        warm = held.tile([P, 1], F32, name="warm")
        nc.scalar.activation(warm[:], eps[:], ACT.Abs_reciprocal_sqrt)

        picked = [[None] * PIECES for b in range(BLOCKS)]
        mean = [None] * PIECES
        diff = [[None] * PIECES for b in range(BLOCKS)]
        variance = [None] * PIECES

        def look_up(b, piece):
            start, width = STARTS[piece], WIDTHS[piece]
            picked[b][piece] = work.tile([P, width], F32, name=f"picked{b}")
            columns = offsets[:, start // 16 : (start + width) // 16]
            nc.scalar.activation(picked[b][piece][:], windows[b][:].indirect(columns), ACT.Copy)

        def open_mean(piece):
            width = WIDTHS[piece]
            mean[piece] = psum_mean.tile([P, width], F32, name="mean")
            if piece < PIECES - 2:
                nc.tensor.matmul(mean[piece][:], averager[:], picked[0][piece][:], start=True, stop=False)
            else:
                rounded = work.tile([P, width], BF16, name="rounded")
                nc.vector.tensor_copy(rounded[:], picked[0][piece][:])
                remainder = work.tile([P, width], BF16, name="remainder")
                nc.vector.tensor_tensor(remainder[:], picked[0][piece][:], rounded[:], ALU.subtract)
                nc.tensor.matmul(mean[piece][:], averager_bf16[:], rounded[:], start=True, stop=False)
                nc.tensor.matmul(mean[piece][:], averager_bf16[:], remainder[:], start=False, stop=False)

        def close_mean(piece):
            nc.tensor.matmul(mean[piece][:], averager[:], picked[1][piece][:], start=False, stop=True)

        def centre(piece):
            for b in range(BLOCKS):
                diff[b][piece] = work.tile([P, WIDTHS[piece]], F32, name=f"diff{b}")
                nc.vector.tensor_tensor(diff[b][piece][:], picked[b][piece][:], mean[piece][:], ALU.subtract)

        def spread(piece):
            variance[piece] = psum_variance.tile([P, WIDTHS[piece]], F32, name="variance")
            for b in range(BLOCKS):
                square = work.tile([P, WIDTHS[piece]], BF16, name=f"square{b}")
                if piece == 0:
                    nc.vector.tensor_tensor(square[:], diff[b][piece][:], diff[b][piece][:], ALU.mult)
                elif piece == 1 and b == 1:
                    nc.gpsimd.tensor_tensor(square[:], diff[b][piece][:], diff[b][piece][:], ALU.mult)
                else:
                    nc.scalar.activation(square[:], diff[b][piece][:], ACT.Square)
                nc.tensor.matmul(
                    variance[piece][:], averager_bf16[:], square[:], start=(b == 0), stop=(b == BLOCKS - 1)
                )

        def normalise(piece):
            start, width = STARTS[piece], WIDTHS[piece]
            rstd = work.tile([P, width], F32, name="rstd")
            nc.scalar.activation(rstd[:], variance[piece][:], ACT.Abs_reciprocal_sqrt, bias=eps[:])
            for b in range(BLOCKS):
                normed = work.tile([P, width], F32, name=f"normed{b}")
                nc.vector.tensor_tensor(normed[:], diff[b][piece][:], rstd[:], ALU.mult)
                nc.sync.dma_start(out[b * P : (b + 1) * P, start : start + width], normed[:])

        last = PIECES - 1
        for piece in range(PIECES):
            look_up(0, piece)
            if piece < last:
                open_mean(piece)
        for piece in range(PIECES):
            look_up(1, piece)
            close_mean(piece)
            if piece == 0:
                open_mean(last)
            centre(piece)
        spread(0)
        for piece in range(1, PIECES):
            spread(piece)
            normalise(piece - 1)
        normalise(PIECES - 1)
